import numpy as np
import ml_dtypes


def mxq(x, axis, fmt="e4m3"):
    dtype, down = {"e4m3": (ml_dtypes.float8_e4m3fn, 7), "e5m2": (ml_dtypes.float8_e5m2, 14)}[fmt]
    v = np.moveaxis(np.asarray(x, np.float32).astype(ml_dtypes.bfloat16).astype(np.float64), axis, -1)
    blocks = v.reshape(v.shape[:-1] + (-1, 32))
    amax = np.abs(blocks).max(-1, keepdims=True)
    byte = np.maximum(np.where(amax > 0, np.frexp(amax)[1] - 1 + 127, 0) - down, 1)
    scale = np.exp2(byte - 127.0)
    codes = (blocks / scale).astype(np.float32).astype(dtype).astype(np.float64)
    return np.moveaxis((codes * scale).reshape(v.shape), -1, axis)


WIDE = False


def mx_kscale(k):
    if not WIDE:
        return np.ones(k)
    levels = np.array([10, -10, 5, -5, 0])
    if k % 512:
        return np.exp2(np.random.permutation(np.resize(levels, k // 32))).repeat(32)
    a = np.empty((k // 512, 16))
    for p in range(k // 512):
        a[p, :8] = np.random.permutation(np.resize(levels, 8))
        for g in range(8):
            far = levels[np.abs(levels - a[p, g]) >= 10]
            a[p, g + 8] = far[np.random.randint(len(far))]
    return np.exp2(a.ravel()).repeat(32)


BF16 = ml_dtypes.bfloat16


def bf(x):
    return np.asarray(x, np.float32).astype(BF16)


def f64(x):
    return np.asarray(x).astype(np.float64)


E2M1 = np.array([0.0, 0.5, 1.0, 1.5, 2.0, 3.0, 4.0, 6.0, -0.0, -0.5, -1.0, -1.5, -2.0, -3.0, -4.0, -6.0])


def pack_weight(w, fmt):
    k, n = w.shape
    w = f64(bf(w)).reshape(k // 32, 32, n)
    amax = np.abs(w).max(1)
    if fmt == "e4m3":
        byte = np.frexp(amax)[1] - 1 + 127 - 7
    else:
        mant, ex = np.frexp(amax / 6.0)
        byte = np.where(mant > 0.5, ex, ex - 1) + 127
    byte = np.clip(np.where(amax > 0, byte, 1), 1, 254)
    scaled = (w * np.exp2(127.0 - byte)[:, None, :]).reshape(k, n).astype(np.float32)
    by_word = np.ascontiguousarray(scaled.reshape(k // 512, 128, 4, n).transpose(0, 1, 3, 2))
    if fmt == "e4m3":
        words = by_word.astype(ml_dtypes.float8_e4m3fn).view(np.uint8)
    else:
        c = by_word.astype(ml_dtypes.float4_e2m1fn).view(np.uint8) & 0xF
        words = c[..., 0::2] | (c[..., 1::2] << 4)
    return np.ascontiguousarray(words), np.ascontiguousarray(byte.astype(np.uint8).reshape(k // 512, 16, n))


def unpack_weight(words, scales, fmt):
    g, p, n, _ = words.shape
    if fmt == "e4m3":
        vals = np.ascontiguousarray(words).view(ml_dtypes.float8_e4m3fn).astype(np.float64)
    else:
        nib = np.empty((g, p, n, 4), np.uint8)
        nib[..., 0::2] = words & 0xF
        nib[..., 1::2] = words >> 4
        vals = E2M1[nib]
    vals = vals * np.repeat(np.exp2(scales.astype(np.float64) - 127.0), 8, axis=1)[..., None]
    return vals.transpose(0, 1, 3, 2).reshape(g * 512, n)
def pack4(w):
    words, scales = pack_weight(w, "e2m1")
    return words.reshape(words.shape[0], 128, -1), scales


def unpack4(words, scales):
    return unpack_weight(words.reshape(words.shape[0], 128, -1, 2), scales, "e2m1")


B, N, C = 64, 16, 512
NEG_SLOPE = 0.2


def leaky(v):
    return np.where(v >= 0, v, NEG_SLOPE * v)


def draw0():
    s, t = mx_kscale(C), mx_kscale(C)
    w1 = np.random.standard_normal((2, C, C)) * 0.7 / np.sqrt(C) / s[None, :, None] * t
    F = bf(np.random.standard_normal((B, N, C)) * s)
    W1_words, W1_scales = pack4(w1.reshape(2 * C, C))
    b1 = bf(np.random.standard_normal(C) * 0.2 * t)
    W2_words, W2_scales = pack4(np.random.standard_normal((C, C)) / np.sqrt(C) / t[:, None])
    b2 = bf(np.random.standard_normal(C) * 0.2)
    return {"F": F,
            "W1_words": W1_words,
            "W1_scales": W1_scales,
            "b1": b1,
            "W2_words": W2_words,
            "W2_scales": W2_scales,
            "b2": b2}


def core(F, W1_words, W1_scales, b1, W2_words, W2_scales, b2):
    Fq = mxq(f64(F), 2, "e4m3")
    W1 = unpack4(W1_words, W1_scales)
    A = Fq @ W1[:C]
    Bp = Fq @ W1[C:]
    h = leaky(A[:, :, None, :] + Bp[:, None, :, :] + f64(b1))
    h = leaky((mxq(h, 3, "e4m3") @ unpack4(W2_words, W2_scales)) + f64(b2))
    return h.sum(-2)


def e4m3fn_bytes(y):
    return np.clip(np.asarray(y, np.float64), -448.0, 448.0).astype(np.float32).astype(ml_dtypes.float8_e4m3fn).view(np.uint8)


def e4m3fn_values(b):
    return np.asarray(b, np.uint8).view(ml_dtypes.float8_e4m3fn).astype(np.float64)


def setup_inputs():
    d = draw0()
    x0 = np.asarray(d['F']).astype(np.float64)
    s = (np.max(np.abs(x0), axis=(0, 1), keepdims=True) / 448.0).astype(np.float32)
    out = {}
    for k, v in d.items():
        if k == 'F':
            out['F_bytes'] = e4m3fn_bytes(x0 / s.astype(np.float64))
            out['F_scale'] = s
        else:
            out[k] = v
    return out


def reference(F_bytes, F_scale, W1_words, W1_scales, b1, W2_words, W2_scales, b2):
    return core(e4m3fn_values(F_bytes) * F_scale.astype(np.float64), W1_words, W1_scales, b1, W2_words, W2_scales, b2)

@@ -1,0 +1,318 @@
+from contextlib import ExitStack
+
+import concourse.mybir as mybir
+from concourse.masks import make_identity
+
+F32 = mybir.dt.float32
+BF16 = mybir.dt.bfloat16
+I32 = mybir.dt.int32
+U8 = mybir.dt.uint8
+FP8 = mybir.dt.float8_e4m3fn
+FP8X4 = mybir.dt.float8_e4m3fn_x4
+FP4X4 = mybir.dt.float4_e2m1fn_x4
+ALU = mybir.AluOpType
+ACT = mybir.ActivationFunctionType
+
+P = 128
+SETS, NODES, C = 64, 16, 512
+SLOPE = 0.2
+FLOPS = 2 * SETS * NODES * C * 2 * C + 2 * SETS * NODES * NODES * C * C
+
+UNIT = 512
+GROUPS = 2
+UNITS = GROUPS * NODES
+AHEAD = 3
+K3 = 256
+KD = UNIT - K3
+
+
+def tile_nonlocalmp_pa_t_w4_kernel(tc, F_bytes, F_scale, W1_words, W1_scales, b1, W2_words, W2_scales, b2, out):
+    nc = tc.nc
+    with ExitStack() as ctx:
+        ctx.enter_context(tc.manual_schedule())
+        const = ctx.enter_context(tc.tile_pool(name="const", bufs=1))
+        work = ctx.enter_context(tc.tile_pool(name="work", bufs=3))
+        ps = ctx.enter_context(tc.psum_pool(name="ps", bufs=1))
+
+        fbytes = const.tile([P, 8 * C], U8, align_bytes=64)
+        f_src = F_bytes.rearrange("b (h m) k -> (b h) (m k)", h=2)
+        nc.sync.dma_start(out=fbytes[:, 0 : 4 * C], in_=f_src[:, 0 : 4 * C])
+        fsc = const.tile([P, 4], F32)
+        nc.sync.dma_start(out=fsc[:], in_=F_scale.rearrange("a c (p t) -> p (a c t)", t=4))
+        w1raw = const.tile([P, 2, 2 * C], U8, align_bytes=64)
+        for g in range(2):
+            nc.sync.dma_start(out=w1raw[:, g, :].bitcast(I32), in_=W1_words[g].bitcast(I32))
+        w1sraw = const.tile([P, 2, C], U8, align_bytes=64)
+        w2s = const.tile([P, C], U8, align_bytes=64)
+        nc.vector.memset(w1sraw[:].rearrange("p g n -> p (g n)").bitcast(I32), 0)
+        nc.vector.memset(w2s[:].bitcast(I32), 0)
+        w1s_src = W1_scales.rearrange("g (q r) n -> r q g n", r=4)
+        w2s_src = W2_scales.rearrange("g (q r) n -> r q (g n)", r=4)
+        for r in range(4):
+            nc.sync.dma_start(out=w1sraw[r:P:32, :, :].bitcast(I32), in_=w1s_src[r].bitcast(I32))
+        b1raw = const.tile([P, 4], BF16)
+        nc.sync.dma_start(out=b1raw[:], in_=b1.rearrange("(p t) -> p t", t=4))
+        nc.sync.dma_start(out=fbytes[:, 4 * C : 8 * C], in_=f_src[:, 4 * C : 8 * C])
+        w2 = const.tile([P, 2 * C], U8, align_bytes=64)
+        nc.sync.dma_start(out=w2[:].bitcast(I32), in_=W2_words[0].bitcast(I32))
+        for r in range(4):
+            nc.sync.dma_start(out=w2s[r:P:32, :].bitcast(I32), in_=w2s_src[r].bitcast(I32))
+        b2raw = const.tile([P, P], BF16)
+        nc.sync.dma_start(out=b2raw[0:4, :], in_=b2.rearrange("(c p) -> c p", p=P))
+
+        ident = const.tile([P, P], F32)
+        make_identity(nc, ident[:])
+        warm = const.tile([P, 1], F32)
+        nc.vector.memset(warm[:], 0.0)
+        nc.scalar.activation(out=warm[:], in_=warm[:], func=ACT.Relu)
+        b2f = const.tile([P, P], F32)
+        nc.vector.memset(b2f[:], 0.0)
+
+        w1p = const.tile([P, 2, 4, 2 * P], U8, align_bytes=64)
+        w1s = const.tile([P, 2, 4, P], U8, align_bytes=64)
+
+        def permute_w1(g):
+            nc.vector.tensor_copy(
+                out=w1p[:, g, :, :].rearrange("p t (m e) -> p t m e", e=2),
+                in_=w1raw[:, g, :].rearrange("p (m t e) -> p t m e", t=4, e=2),
+            )
+
+        def permute_w1_scales(g):
+            nc.vector.tensor_copy(out=w1s[:, g, :, :], in_=w1sraw[:, g, :].rearrange("p (m t) -> p t m", t=4))
+
+        fwide = const.tile([P, 8, C], BF16, align_bytes=64)
+        fg = const.tile([P, NODES, SETS, 4], BF16, align_bytes=64)
+        fq = const.tile([P, NODES, SETS], I32, align_bytes=64)
+        fs = const.tile([P, NODES, SETS], U8, align_bytes=64)
+        f8q = const.tile([P, NODES, 8, SETS], I32, align_bytes=64)
+        f8s = const.tile([P, NODES, 8, SETS], U8, align_bytes=64)
+
+        def widen(m):
+            nc.scalar.copy(out=fwide[:, m, :], in_=fbytes[:, m * C : (m + 1) * C].bitcast(FP8))
+
+        def transpose_pair(m, tag):
+            xt = ps.tile([P, 2, 2, P], F32, name="xt", tag=tag)
+            for mm in range(2):
+                words = fwide[:, m + mm, :].bitcast(F32)
+                for u in range(2):
+                    nc.tensor.transpose(xt[:, mm, u, :], words[:, u::2], ident[:])
+            return xt
+
+        def scale_out(xt, m):
+            for mm in range(2):
+                src = xt[:, mm, :, :].bitcast(BF16).rearrange("p u (b h e) -> p h b u e", h=2, e=2)
+                sc = fsc[:].rearrange("p (o u e) -> p o u e", o=1, u=2).to_broadcast([P, SETS, 2, 2])
+                for h in range(2):
+                    nc.vector.tensor_tensor(
+                        out=fg[:, 2 * (m + mm) + h, :, :].rearrange("p b (u e) -> p b u e", e=2),
+                        in0=src[:, h],
+                        in1=sc,
+                        op=ALU.mult,
+                    )
+
+        def quantise_f(g):
+            jj = slice(8 * g, 8 * g + 8)
+            nc.vector.quantize_mx(
+                out=fq[:, jj, :].rearrange("p j b -> p (j b)").bitcast(FP8X4),
+                scales=fs[:, jj, :].rearrange("p j b -> p (j b)"),
+                in_=fg[:, jj, :, :].rearrange("p j b t -> p (j b t)"),
+            )
+
+        def repeat_f(j0, j1):
+            n = j1 - j0
+            nc.vector.tensor_copy(
+                out=f8q[:, j0:j1, :, :],
+                in_=fq[:, j0:j1, :].unsqueeze(2).to_broadcast([P, n, 8, SETS]),
+            )
+            nc.vector.tensor_copy(
+                out=f8s[:, j0:j1, :, :].bitcast(I32),
+                in_=fs[:, j0:j1, :].bitcast(I32).unsqueeze(2).to_broadcast([P, n, 8, SETS // 4]),
+            )
+
+        for m in range(4):
+            widen(m)
+        xt0 = transpose_pair(0, "l0")
+        xt1 = transpose_pair(2, "l1")
+        permute_w1(0)
+        permute_w1(1)
+        scale_out(xt0, 0)
+        scale_out(xt1, 2)
+        quantise_f(0)
+        repeat_f(0, 2)
+        permute_w1_scales(0)
+        permute_w1_scales(1)
+        b1f = const.tile([P, 4], F32)
+        nc.vector.tensor_copy(out=b1f[:], in_=b1raw[:])
+        for m in range(4, 8):
+            widen(m)
+
+        def late_setup():
+            xt2 = transpose_pair(4, "l2")
+            xt3 = transpose_pair(6, "l3")
+            scale_out(xt2, 4)
+            scale_out(xt3, 6)
+            quantise_f(1)
+
+        nb2 = const.tile([P, 4], F32)
+        b2x20 = const.tile([P, 4], F32)
+
+        def setup_b2():
+            nc.vector.tensor_copy(out=b2f[0:4, :], in_=b2raw[0:4, :])
+            bt = ps.tile([P, P], F32, name="bt", tag="l0")
+            nc.tensor.transpose(bt[:], b2f[:], ident[:])
+            nc.vector.tensor_scalar(out=nb2[:], in0=bt[:, 0:4], scalar1=-1.0, scalar2=None, op0=ALU.mult)
+            nc.vector.tensor_scalar(out=b2x20[:], in0=bt[:, 0:4], scalar1=20.0, scalar2=None, op0=ALU.mult)
+
+        v_of, h_of, hq_of, pn_of, acc_of, lin_of = {}, {}, {}, {}, {}, {}
+
+        def first_matmul(u, t):
+            g, j = divmod(u, NODES)
+            z = ps.tile([P, UNIT], F32, name="z", tag="z", bufs=2)
+            jj = slice(8 * g, 8 * g + 8)
+            nc.tensor.matmul_mx(
+                out=z[:],
+                lhsT=w1p[:, 0, t, :].bitcast(FP4X4),
+                lhsT_scale=w1s[:, 0, t, :],
+                rhs=fq[:, jj, :].rearrange("p j b -> p (j b)").bitcast(FP8X4),
+                rhs_scale=fs[:, jj, :].rearrange("p j b -> p (j b)"),
+                start=True,
+                stop=False,
+            )
+            nc.tensor.matmul_mx(
+                out=z[:],
+                lhsT=w1p[:, 1, t, :].bitcast(FP4X4),
+                lhsT_scale=w1s[:, 1, t, :],
+                rhs=f8q[:, j, :, :].rearrange("p r b -> p (r b)").bitcast(FP8X4),
+                rhs_scale=f8s[:, j, :, :].rearrange("p r b -> p (r b)"),
+                start=False,
+                stop=True,
+            )
+            return z
+
+        def leave_first(u, t, z):
+            if t == 0:
+                v = work.tile([P, 4, UNIT], F32, name="v")
+                v_of[u] = v
+            nc.scalar.activation(out=v_of[u][:, t, :], in_=z[:], func=ACT.Identity, bias=b1f[:, t : t + 1], scale=1.0)
+
+        def positive_part(u):
+            pos = work.tile([P, K3, 4], BF16, name="pos", bufs=2)
+            neg = work.tile([P, K3, 4], BF16, name="neg", bufs=2)
+            pn_of[u] = (pos, neg)
+            nc.scalar.activation(out=pos[:], in_=v_of[u][:, :, KD:].rearrange("p t n -> p n t"), func=ACT.Relu)
+
+        def negative_part(u):
+            nc.scalar.activation(out=pn_of[u][1][:], in_=v_of[u][:, :, KD:].rearrange("p t n -> p n t"), func=ACT.Relu, scale=-SLOPE)
+
+        def leaky_direct(u, n0, n1):
+            if n0 == 0:
+                h = work.tile([P, UNIT, 4], BF16, name="h", align_bytes=64)
+                h_of[u] = h
+            src = v_of[u][:, :, n0:n1].rearrange("p t n -> p n t")
+            nc.vector.scalar_tensor_tensor(out=h_of[u][:, n0:n1, :], in0=src, scalar=SLOPE, in1=src, op0=ALU.mult, op1=ALU.max)
+
+        def leaky_join(u):
+            pos, neg = pn_of.pop(u)
+            nc.vector.tensor_tensor(out=h_of[u][:, KD:, :], in0=pos[:], in1=neg[:], op=ALU.subtract)
+
+        def quantise_h(u):
+            hq = work.tile([P, UNIT], I32, name="hq", align_bytes=64)
+            hs = work.tile([P, UNIT], U8, name="hs", align_bytes=64)
+            hq_of[u] = (hq, hs)
+            nc.vector.quantize_mx(out=hq[:].bitcast(FP8X4), scales=hs[:], in_=h_of.pop(u)[:].rearrange("p n t -> p (n t)"))
+
+        def second_matmul(u, c, to, start, stop):
+            hq, hs = hq_of[u]
+            nc.tensor.matmul_mx(
+                out=to[:],
+                lhsT=w2[:, 2 * P * c : 2 * P * (c + 1)].bitcast(FP4X4),
+                lhsT_scale=w2s[:, P * c : P * (c + 1)],
+                rhs=hq[:].bitcast(FP8X4),
+                rhs_scale=hs[:],
+                start=start,
+                stop=stop,
+            )
+
+        def message(u, c):
+            r = ps.tile([P, UNIT], F32, name="r", tag="r", bufs=2)
+            second_matmul(u, c, r, True, True)
+            return r
+
+        def linear_sum(u, c):
+            g, j = divmod(u, NODES)
+            if j == 0:
+                lin = ps.tile([P, UNIT], F32, name="lin", tag="l%d" % c)
+                lin_of[g, c] = lin
+            second_matmul(u, c, lin_of[g, c], j == 0, j == NODES - 1)
+
+        def accumulate(u, c, r):
+            g, j = divmod(u, NODES)
+            if j == 0 and c == 0:
+                acc = const.tile([P, 4, UNIT], F32, name="acc%d" % g)
+                acc_of[g] = acc
+            a = acc_of[g][:, c, :]
+            if j == 0:
+                nc.vector.tensor_scalar(out=a, in0=r[:], scalar1=nb2[:, c : c + 1], scalar2=b2x20[:, c : c + 1], op0=ALU.max, op1=ALU.add)
+            else:
+                nc.vector.scalar_tensor_tensor(out=a, in0=r[:], scalar=nb2[:, c : c + 1], in1=a, op0=ALU.max, op1=ALU.add)
+
+        def fold(g, c):
+            a = acc_of[g][:, c, :]
+            nc.vector.scalar_tensor_tensor(out=a, in0=lin_of[g, c][:], scalar=0.25, in1=a, op0=ALU.mult, op1=ALU.add)
+
+        out_v = out.rearrange("b (h q s) c -> h q b s c", h=2, q=2)
+
+        def finish(g, c, tag, bufs, on_vector):
+            tr = ps.tile([P, 4, P], F32, name="tr", tag=tag, bufs=bufs)
+            for s in range(4):
+                nc.tensor.transpose(tr[:, s, :], acc_of[g][:, c, P * s : P * (s + 1)], ident[:])
+            st = work.tile([P, 4, P], F32, name="st")
+            if on_vector:
+                nc.vector.tensor_scalar(out=st[:], in0=tr[:], scalar1=0.8, scalar2=None, op0=ALU.mult)
+            else:
+                nc.scalar.activation(out=st[:], in_=tr[:], func=ACT.Copy, scale=0.8)
+            for h in range(2):
+                nc.sync.dma_start(out=out_v[h, g][:, :, P * c : P * (c + 1)], in_=st[64 * h : 64 * h + 64, :, :])
+
+        for u in range(-AHEAD, UNITS):
+            if u == -2:
+                late_setup()
+            if u == -1:
+                setup_b2()
+                repeat_f(2, 4)
+            if u >= 0 and u < 12 and u % 2 == 0:
+                repeat_f(u + 4, u + 6)
+            w = u + AHEAD
+            for c in range(4):
+                if u >= 0:
+                    r = message(u, c)
+                    linear_sum(u, c)
+                if w < UNITS:
+                    z = first_matmul(w, c)
+                if 0 <= w - 1 < UNITS:
+                    if c == 0:
+                        positive_part(w - 1)
+                    if c == 1:
+                        negative_part(w - 1)
+                if w < UNITS:
+                    leave_first(w, c, z)
+                if u >= 0:
+                    accumulate(u, c, r)
+                if c == 0 and 0 <= u + 1 < UNITS:
+                    quantise_h(u + 1)
+                if 0 <= w - 1 < UNITS:
+                    if c == 1:
+                        leaky_direct(w - 1, 0, KD // 2)
+                    if c == 2:
+                        leaky_direct(w - 1, KD // 2, KD)
+                    if c == 3:
+                        leaky_join(w - 1)
+                if u >= 0 and u % NODES == NODES - 1:
+                    if c > 0:
+                        fold(u // NODES, c - 1)
+                    if c == 3:
+                        fold(u // NODES, 3)
+                if NODES <= u < NODES + 4 and c == 3:
+                    finish(0, u - NODES, "r", 2, False)
+        for c in range(4):
+            finish(1, c, ("r", "z")[c % 2], 2, c % 2 == 1)

@@ -78,7 +78,7 @@ def tile_nonlocalmp_pa_t_w4_kernel(tc, F_bytes, F_scale, W1_words, W1_scales, b1
             )
 
         def permute_w1_scales(g):
-            nc.vector.tensor_copy(out=w1s[:, g, :, :], in_=w1sraw[:, g, :].rearrange("p (m t) -> p t m", t=4))
+            nc.gpsimd.tensor_copy(out=w1s[:, g, :, :], in_=w1sraw[:, g, :].rearrange("p (m t) -> p t m", t=4))
 
         fwide = const.tile([P, 8, C], BF16, align_bytes=64)
         fg = const.tile([P, NODES, SETS, 4], BF16, align_bytes=64)
@@ -129,6 +129,8 @@ def tile_nonlocalmp_pa_t_w4_kernel(tc, F_bytes, F_scale, W1_words, W1_scales, b1
                 in_=fs[:, j0:j1, :].bitcast(I32).unsqueeze(2).to_broadcast([P, n, 8, SETS // 4]),
             )
 
+        permute_w1_scales(0)
+        permute_w1_scales(1)
         for m in range(4):
             widen(m)
         xt0 = transpose_pair(0, "l0")
@@ -138,14 +140,10 @@ def tile_nonlocalmp_pa_t_w4_kernel(tc, F_bytes, F_scale, W1_words, W1_scales, b1
         scale_out(xt0, 0)
         scale_out(xt1, 2)
         quantise_f(0)
-        repeat_f(0, 2)
-        permute_w1_scales(0)
-        permute_w1_scales(1)
+        repeat_f(0, 1)
+        repeat_f(1, 2)
         b1f = const.tile([P, 4], F32)
         nc.vector.tensor_copy(out=b1f[:], in_=b1raw[:])
-        for m in range(4, 8):
-            widen(m)
-
         def late_setup():
             xt2 = transpose_pair(4, "l2")
             xt3 = transpose_pair(6, "l3")
@@ -191,35 +189,35 @@ def tile_nonlocalmp_pa_t_w4_kernel(tc, F_bytes, F_scale, W1_words, W1_scales, b1
 
         def leave_first(u, t, z):
             if t == 0:
-                v = work.tile([P, 4, UNIT], F32, name="v")
+                v = work.tile([P, UNIT // 4, 4, 4], F32, name="v", align_bytes=64)
                 v_of[u] = v
-            nc.scalar.activation(out=v_of[u][:, t, :], in_=z[:], func=ACT.Identity, bias=b1f[:, t : t + 1], scale=1.0)
+            nc.scalar.activation(out=v_of[u][:, :, t, :], in_=z[:].rearrange("p (e c) -> p c e", e=4), func=ACT.Identity, bias=b1f[:, t : t + 1], scale=1.0)
 
         def positive_part(u):
-            pos = work.tile([P, K3, 4], BF16, name="pos", bufs=2)
-            neg = work.tile([P, K3, 4], BF16, name="neg", bufs=2)
+            pos = work.tile([P, 4, K3 // 4, 4], BF16, name="pos", bufs=2)
+            neg = work.tile([P, 4, K3 // 4, 4], BF16, name="neg", bufs=2)
             pn_of[u] = (pos, neg)
-            nc.scalar.activation(out=pos[:], in_=v_of[u][:, :, KD:].rearrange("p t n -> p n t"), func=ACT.Relu)
+            nc.scalar.activation(out=pos[:].rearrange("p e c t -> p (c t) e"), in_=v_of[u][:, KD // 4 :].rearrange("p c t e -> p (c t) e"), func=ACT.Relu)
 
         def negative_part(u):
-            nc.scalar.activation(out=pn_of[u][1][:], in_=v_of[u][:, :, KD:].rearrange("p t n -> p n t"), func=ACT.Relu, scale=-SLOPE)
+            nc.scalar.activation(out=pn_of[u][1][:].rearrange("p e c t -> p (c t) e"), in_=v_of[u][:, KD // 4 :].rearrange("p c t e -> p (c t) e"), func=ACT.Relu, scale=-SLOPE)
 
         def leaky_direct(u, n0, n1):
             if n0 == 0:
-                h = work.tile([P, UNIT, 4], BF16, name="h", align_bytes=64)
+                h = work.tile([P, 4, UNIT // 4, 4], BF16, name="h", align_bytes=64)
                 h_of[u] = h
-            src = v_of[u][:, :, n0:n1].rearrange("p t n -> p n t")
-            nc.vector.scalar_tensor_tensor(out=h_of[u][:, n0:n1, :], in0=src, scalar=SLOPE, in1=src, op0=ALU.mult, op1=ALU.max)
+            src = v_of[u][:, n0 // 4 : n1 // 4].rearrange("p c t e -> p (c t) e")
+            nc.vector.scalar_tensor_tensor(out=h_of[u][:, :, n0 // 4 : n1 // 4, :].rearrange("p e c t -> p (c t) e"), in0=src, scalar=SLOPE, in1=src, op0=ALU.mult, op1=ALU.max)
 
         def leaky_join(u):
             pos, neg = pn_of.pop(u)
-            nc.vector.tensor_tensor(out=h_of[u][:, KD:, :], in0=pos[:], in1=neg[:], op=ALU.subtract)
+            nc.vector.tensor_tensor(out=h_of[u][:, :, KD // 4 :, :], in0=pos[:], in1=neg[:], op=ALU.subtract)
 
         def quantise_h(u):
             hq = work.tile([P, UNIT], I32, name="hq", align_bytes=64)
             hs = work.tile([P, UNIT], U8, name="hs", align_bytes=64)
             hq_of[u] = (hq, hs)
-            nc.vector.quantize_mx(out=hq[:].bitcast(FP8X4), scales=hs[:], in_=h_of.pop(u)[:].rearrange("p n t -> p (n t)"))
+            nc.vector.quantize_mx(out=hq[:].bitcast(FP8X4), scales=hs[:], in_=h_of.pop(u)[:].rearrange("p e c t -> p (e c t)"))
 
         def second_matmul(u, c, to, start, stop):
             hq, hs = hq_of[u]
@@ -275,9 +273,8 @@ def tile_nonlocalmp_pa_t_w4_kernel(tc, F_bytes, F_scale, W1_words, W1_scales, b1
                 nc.sync.dma_start(out=out_v[h, g][:, :, P * c : P * (c + 1)], in_=st[64 * h : 64 * h + 64, :, :])
 
         for u in range(-AHEAD, UNITS):
-            if u == -2:
-                late_setup()
             if u == -1:
+                late_setup()
                 setup_b2()
                 repeat_f(2, 4)
             if u >= 0 and u < 12 and u % 2 == 0:
@@ -312,6 +309,9 @@ def tile_nonlocalmp_pa_t_w4_kernel(tc, F_bytes, F_scale, W1_words, W1_scales, b1
                         fold(u // NODES, c - 1)
                     if c == 3:
                         fold(u // NODES, 3)
+                if u == -3 and c == 3:
+                    for m in range(4, 8):
+                        widen(m)
                 if NODES <= u < NODES + 4 and c == 3:
                     finish(0, u - NODES, "r", 2, False)
         for c in range(4):

@@ -22,8 +22,12 @@ UNIT = 512
 GROUPS = 2
 UNITS = GROUPS * NODES
 AHEAD = 3
-K3 = 256
-KD = UNIT - K3
+BLOCK = UNIT // 4
+SPLIT = [0, 0, 32] + [60] * 29
+
+
+def on_scalar(u):
+    return SPLIT[u]
 
 
 def tile_nonlocalmp_pa_t_w4_kernel(tc, F_bytes, F_scale, W1_words, W1_scales, b1, W2_words, W2_scales, b2, out):
@@ -40,8 +44,6 @@ def tile_nonlocalmp_pa_t_w4_kernel(tc, F_bytes, F_scale, W1_words, W1_scales, b1
         fsc = const.tile([P, 4], F32)
         nc.sync.dma_start(out=fsc[:], in_=F_scale.rearrange("a c (p t) -> p (a c t)", t=4))
         w1raw = const.tile([P, 2, 2 * C], U8, align_bytes=64)
-        for g in range(2):
-            nc.sync.dma_start(out=w1raw[:, g, :].bitcast(I32), in_=W1_words[g].bitcast(I32))
         w1sraw = const.tile([P, 2, C], U8, align_bytes=64)
         w2s = const.tile([P, C], U8, align_bytes=64)
         nc.vector.memset(w1sraw[:].rearrange("p g n -> p (g n)").bitcast(I32), 0)
@@ -50,6 +52,8 @@ def tile_nonlocalmp_pa_t_w4_kernel(tc, F_bytes, F_scale, W1_words, W1_scales, b1
         w2s_src = W2_scales.rearrange("g (q r) n -> r q (g n)", r=4)
         for r in range(4):
             nc.sync.dma_start(out=w1sraw[r:P:32, :, :].bitcast(I32), in_=w1s_src[r].bitcast(I32))
+        for g in range(2):
+            nc.sync.dma_start(out=w1raw[:, g, :].bitcast(I32), in_=W1_words[g].bitcast(I32))
         b1raw = const.tile([P, 4], BF16)
         nc.sync.dma_start(out=b1raw[:], in_=b1.rearrange("(p t) -> p t", t=4))
         nc.sync.dma_start(out=fbytes[:, 4 * C : 8 * C], in_=f_src[:, 4 * C : 8 * C])
@@ -59,6 +63,8 @@ def tile_nonlocalmp_pa_t_w4_kernel(tc, F_bytes, F_scale, W1_words, W1_scales, b1
             nc.sync.dma_start(out=w2s[r:P:32, :].bitcast(I32), in_=w2s_src[r].bitcast(I32))
         b2raw = const.tile([P, P], BF16)
         nc.sync.dma_start(out=b2raw[0:4, :], in_=b2.rearrange("(c p) -> c p", p=P))
+        fsc_all = const.tile([P, C], F32)
+        nc.sync.dma_start(out=fsc_all[:], in_=F_scale.rearrange("a c k -> (a c k)").partition_broadcast(P))
 
         ident = const.tile([P, P], F32)
         make_identity(nc, ident[:])
@@ -66,15 +72,15 @@ def tile_nonlocalmp_pa_t_w4_kernel(tc, F_bytes, F_scale, W1_words, W1_scales, b1
         nc.vector.memset(warm[:], 0.0)
         nc.scalar.activation(out=warm[:], in_=warm[:], func=ACT.Relu)
         b2f = const.tile([P, P], F32)
-        nc.vector.memset(b2f[:], 0.0)
+        nc.gpsimd.memset(b2f[:], 0.0)
 
         w1p = const.tile([P, 2, 4, 2 * P], U8, align_bytes=64)
         w1s = const.tile([P, 2, 4, P], U8, align_bytes=64)
 
-        def permute_w1(g):
-            nc.vector.tensor_copy(
-                out=w1p[:, g, :, :].rearrange("p t (m e) -> p t m e", e=2),
-                in_=w1raw[:, g, :].rearrange("p (m t e) -> p t m e", t=4, e=2),
+        def permute_w1(engine, g, t0, t1):
+            engine.tensor_copy(
+                out=w1p[:, g, t0:t1, :].rearrange("p t (m e) -> p t m e", e=2),
+                in_=w1raw[:, g, :].rearrange("p (m t e) -> p t m e", t=4, e=2)[:, t0:t1],
             )
 
         def permute_w1_scales(g):
@@ -131,41 +137,68 @@ def tile_nonlocalmp_pa_t_w4_kernel(tc, F_bytes, F_scale, W1_words, W1_scales, b1
 
         permute_w1_scales(0)
         permute_w1_scales(1)
-        for m in range(4):
+        def repeat_f_dma(j0, j1):
+            for j in range(j0, j1):
+                nc.sync.dma_start(out=f8q[:, j, :, :], in_=fq[:, j, :].unsqueeze(1).to_broadcast([P, 8, SETS]))
+                nc.sync.dma_start(
+                    out=f8s[:, j, :, :].bitcast(I32),
+                    in_=fs[:, j, :].bitcast(I32).unsqueeze(1).to_broadcast([P, 8, SETS // 4]),
+                )
+
+        fscaled = const.tile([P, 4, C], BF16, align_bytes=64)
+
+        def transpose_scaled_pair(m, tag):
+            for mm in range(2):
+                nc.gpsimd.tensor_tensor(out=fscaled[:, m + mm - 4, :], in0=fwide[:, m + mm, :], in1=fsc_all[:], op=ALU.mult)
+            xt = ps.tile([P, 2, 2, P], F32, name="xt", tag=tag)
+            for mm in range(2):
+                words = fscaled[:, m + mm - 4, :].bitcast(F32)
+                for u in range(2):
+                    nc.tensor.transpose(xt[:, mm, u, :], words[:, u::2], ident[:])
+            return xt
+
+        def words_out(xt, m):
+            for mm in range(2):
+                jj = 2 * (m + mm)
+                nc.scalar.copy(
+                    out=fg[:, jj : jj + 2, :, :].bitcast(F32),
+                    in_=xt[:, mm, :, :].rearrange("p u (b h) -> p h b u", h=2),
+                )
+
+        for m in (2, 3):
+            nc.vector.tensor_copy(out=fwide[:, m, :], in_=fbytes[:, m * C : (m + 1) * C].bitcast(FP8))
+        for m in (0, 1):
             widen(m)
         xt0 = transpose_pair(0, "l0")
         xt1 = transpose_pair(2, "l1")
-        permute_w1(0)
-        permute_w1(1)
         scale_out(xt0, 0)
         scale_out(xt1, 2)
         quantise_f(0)
+        for g in range(2):
+            permute_w1(nc.vector, g, 0, 2)
         repeat_f(0, 1)
+        for g in range(2):
+            permute_w1(nc.vector, g, 2, 4)
+        for m in range(4, 8):
+            widen(m)
         repeat_f(1, 2)
-        b1f = const.tile([P, 4], F32)
-        nc.vector.tensor_copy(out=b1f[:], in_=b1raw[:])
-        def late_setup():
-            xt2 = transpose_pair(4, "l2")
-            xt3 = transpose_pair(6, "l3")
-            scale_out(xt2, 4)
-            scale_out(xt3, 6)
-            quantise_f(1)
-
+        repeat_f_dma(2, 4)
+        repeat_f_dma(4, 8)
         nb2 = const.tile([P, 4], F32)
         b2x20 = const.tile([P, 4], F32)
 
         def setup_b2():
-            nc.vector.tensor_copy(out=b2f[0:4, :], in_=b2raw[0:4, :])
+            nc.scalar.copy(out=b2f[0:4, :], in_=b2raw[0:4, :])
             bt = ps.tile([P, P], F32, name="bt", tag="l0")
             nc.tensor.transpose(bt[:], b2f[:], ident[:])
-            nc.vector.tensor_scalar(out=nb2[:], in0=bt[:, 0:4], scalar1=-1.0, scalar2=None, op0=ALU.mult)
-            nc.vector.tensor_scalar(out=b2x20[:], in0=bt[:, 0:4], scalar1=20.0, scalar2=None, op0=ALU.mult)
+            nc.scalar.activation(out=nb2[:], in_=bt[:, 0:4], func=ACT.Copy, scale=-1.0)
+            nc.scalar.activation(out=b2x20[:], in_=bt[:, 0:4], func=ACT.Copy, scale=20.0)
 
         v_of, h_of, hq_of, pn_of, acc_of, lin_of = {}, {}, {}, {}, {}, {}
 
-        def first_matmul(u, t):
+        def first_matmul(u, t, tag="z"):
             g, j = divmod(u, NODES)
-            z = ps.tile([P, UNIT], F32, name="z", tag="z", bufs=2)
+            z = ps.tile([P, UNIT], F32, name="z", tag=tag, bufs=2)
             jj = slice(8 * g, 8 * g + 8)
             nc.tensor.matmul_mx(
                 out=z[:],
@@ -191,27 +224,39 @@ def tile_nonlocalmp_pa_t_w4_kernel(tc, F_bytes, F_scale, W1_words, W1_scales, b1
             if t == 0:
                 v = work.tile([P, UNIT // 4, 4, 4], F32, name="v", align_bytes=64)
                 v_of[u] = v
-            nc.scalar.activation(out=v_of[u][:, :, t, :], in_=z[:].rearrange("p (e c) -> p c e", e=4), func=ACT.Identity, bias=b1f[:, t : t + 1], scale=1.0)
+            nc.scalar.activation(out=v_of[u][:, :, t, :], in_=z[:].rearrange("p (e c) -> p c e", e=4), func=ACT.Identity, bias=b1raw[:, t : t + 1], scale=1.0)
 
-        def positive_part(u):
-            pos = work.tile([P, 4, K3 // 4, 4], BF16, name="pos", bufs=2)
-            neg = work.tile([P, 4, K3 // 4, 4], BF16, name="neg", bufs=2)
-            pn_of[u] = (pos, neg)
-            nc.scalar.activation(out=pos[:].rearrange("p e c t -> p (c t) e"), in_=v_of[u][:, KD // 4 :].rearrange("p c t e -> p (c t) e"), func=ACT.Relu)
-
-        def negative_part(u):
-            nc.scalar.activation(out=pn_of[u][1][:].rearrange("p e c t -> p (c t) e"), in_=v_of[u][:, KD // 4 :].rearrange("p c t e -> p (c t) e"), func=ACT.Relu, scale=-SLOPE)
+        def scalar_part(u, piece, pieces):
+            k = on_scalar(u)
+            if k == 0:
+                return
+            if piece == 0:
+                pos = work.tile([P, 4, BLOCK, 4], BF16, name="pos", bufs=2)
+                neg = work.tile([P, 4, BLOCK, 4], BF16, name="neg", bufs=2)
+                pn_of[u] = (pos, neg)
+            sign, part = divmod(piece, pieces // 2)
+            n = k // (pieces // 2)
+            lo = part * n
+            nc.scalar.activation(
+                out=pn_of[u][sign][:, :, lo : lo + n, :].rearrange("p e c t -> p (c t) e"),
+                in_=v_of[u][:, BLOCK - k + lo : BLOCK - k + lo + n].rearrange("p c t e -> p (c t) e"),
+                func=ACT.Relu,
+                scale=(1.0, -SLOPE)[sign],
+            )
 
         def leaky_direct(u, n0, n1):
             if n0 == 0:
                 h = work.tile([P, 4, UNIT // 4, 4], BF16, name="h", align_bytes=64)
                 h_of[u] = h
-            src = v_of[u][:, n0 // 4 : n1 // 4].rearrange("p c t e -> p (c t) e")
-            nc.vector.scalar_tensor_tensor(out=h_of[u][:, :, n0 // 4 : n1 // 4, :].rearrange("p e c t -> p (c t) e"), in0=src, scalar=SLOPE, in1=src, op0=ALU.mult, op1=ALU.max)
+            src = v_of[u][:, n0:n1].rearrange("p c t e -> p (c t) e")
+            nc.vector.scalar_tensor_tensor(out=h_of[u][:, :, n0:n1, :].rearrange("p e c t -> p (c t) e"), in0=src, scalar=SLOPE, in1=src, op0=ALU.mult, op1=ALU.max)
 
         def leaky_join(u):
+            k = on_scalar(u)
+            if k == 0:
+                return
             pos, neg = pn_of.pop(u)
-            nc.vector.tensor_tensor(out=h_of[u][:, :, KD // 4 :, :], in0=pos[:], in1=neg[:], op=ALU.subtract)
+            nc.vector.tensor_tensor(out=h_of[u][:, :, BLOCK - k :, :], in0=pos[:, :, 0:k, :], in1=neg[:, :, 0:k, :], op=ALU.subtract)
 
         def quantise_h(u):
             hq = work.tile([P, UNIT], I32, name="hq", align_bytes=64)
@@ -254,16 +299,21 @@ def tile_nonlocalmp_pa_t_w4_kernel(tc, F_bytes, F_scale, W1_words, W1_scales, b1
             else:
                 nc.vector.scalar_tensor_tensor(out=a, in0=r[:], scalar=nb2[:, c : c + 1], in1=a, op0=ALU.max, op1=ALU.add)
 
-        def fold(g, c):
-            a = acc_of[g][:, c, :]
-            nc.vector.scalar_tensor_tensor(out=a, in0=lin_of[g, c][:], scalar=0.25, in1=a, op0=ALU.mult, op1=ALU.add)
+        quarter_of = {}
+
+        def leave_linear(g, c):
+            quarter = work.tile([P, UNIT], F32, name="quarter", bufs=4)
+            nc.scalar.activation(out=quarter[:], in_=lin_of[g, c][:], func=ACT.Copy, scale=0.25)
+            quarter_of[g, c] = quarter
 
         out_v = out.rearrange("b (h q s) c -> h q b s c", h=2, q=2)
 
         def finish(g, c, tag, bufs, on_vector):
             tr = ps.tile([P, 4, P], F32, name="tr", tag=tag, bufs=bufs)
             for s in range(4):
-                nc.tensor.transpose(tr[:, s, :], acc_of[g][:, c, P * s : P * (s + 1)], ident[:])
+                cols = slice(P * s, P * (s + 1))
+                nc.tensor.matmul(tr[:, s, :], lhsT=quarter_of[g, c][:, cols], rhs=ident[:], is_transpose=True, start=True, stop=False)
+                nc.tensor.matmul(tr[:, s, :], lhsT=acc_of[g][:, c, cols], rhs=ident[:], is_transpose=True, start=False, stop=True)
             st = work.tile([P, 4, P], F32, name="st")
             if on_vector:
                 nc.vector.tensor_scalar(out=st[:], in0=tr[:], scalar1=0.8, scalar2=None, op0=ALU.mult)
@@ -272,46 +322,60 @@ def tile_nonlocalmp_pa_t_w4_kernel(tc, F_bytes, F_scale, W1_words, W1_scales, b1
             for h in range(2):
                 nc.sync.dma_start(out=out_v[h, g][:, :, P * c : P * (c + 1)], in_=st[64 * h : 64 * h + 64, :, :])
 
-        for u in range(-AHEAD, UNITS):
-            if u == -1:
-                late_setup()
-                setup_b2()
-                repeat_f(2, 4)
-            if u >= 0 and u < 12 and u % 2 == 0:
-                repeat_f(u + 4, u + 6)
+        def unit_matmuls(u):
+            for t in range(4):
+                z = first_matmul(u, t, "zr"[t % 2])
+                leave_first(u, t, z)
+
+        def halves(u):
+            d = BLOCK - on_scalar(u)
+            return d // 2, d
+
+        setup_b2()
+        unit_matmuls(0)
+        leaky_direct(0, 0, BLOCK)
+        unit_matmuls(1)
+        scalar_part(1, 0, 2)
+        scalar_part(1, 1, 2)
+        quantise_h(0)
+        unit_matmuls(2)
+        xt2 = transpose_scaled_pair(4, "l2")
+        xt3 = transpose_scaled_pair(6, "l3")
+        leaky_direct(1, 0, halves(1)[1])
+        leaky_join(1)
+
+        for u in range(UNITS):
+            if u == 1:
+                quantise_f(1)
+                repeat_f_dma(8, 12)
+                repeat_f_dma(12, 16)
             w = u + AHEAD
             for c in range(4):
-                if u >= 0:
-                    r = message(u, c)
-                    linear_sum(u, c)
                 if w < UNITS:
                     z = first_matmul(w, c)
-                if 0 <= w - 1 < UNITS:
-                    if c == 0:
-                        positive_part(w - 1)
-                    if c == 1:
-                        negative_part(w - 1)
+                r = message(u, c)
+                linear_sum(u, c)
+                if w - 1 < UNITS:
+                    scalar_part(w - 1, c, 4)
                 if w < UNITS:
                     leave_first(w, c, z)
-                if u >= 0:
-                    accumulate(u, c, r)
-                if c == 0 and 0 <= u + 1 < UNITS:
+                if u == 0 and c == 0:
+                    words_out(xt2, 4)
+                if u == 0 and c == 1:
+                    words_out(xt3, 6)
+                accumulate(u, c, r)
+                if c == 1 and u + 1 < UNITS:
                     quantise_h(u + 1)
-                if 0 <= w - 1 < UNITS:
-                    if c == 1:
-                        leaky_direct(w - 1, 0, KD // 2)
+                if w - 1 < UNITS:
+                    a, b = halves(w - 1)
+                    if c == 0:
+                        leaky_direct(w - 1, 0, a)
                     if c == 2:
-                        leaky_direct(w - 1, KD // 2, KD)
+                        leaky_direct(w - 1, a, b)
                     if c == 3:
                         leaky_join(w - 1)
-                if u >= 0 and u % NODES == NODES - 1:
-                    if c > 0:
-                        fold(u // NODES, c - 1)
-                    if c == 3:
-                        fold(u // NODES, 3)
-                if u == -3 and c == 3:
-                    for m in range(4, 8):
-                        widen(m)
+                if u % NODES == NODES - 1:
+                    leave_linear(u // NODES, c)
                 if NODES <= u < NODES + 4 and c == 3:
                     finish(0, u - NODES, "r", 2, False)
         for c in range(4):

@@ -23,7 +23,7 @@ GROUPS = 2
 UNITS = GROUPS * NODES
 AHEAD = 3
 BLOCK = UNIT // 4
-SPLIT = [0, 0, 32] + [60] * 29
+SPLIT = [0, 0, 32] + [58] * 29
 
 
 def on_scalar(u):
@@ -44,6 +44,8 @@ def tile_nonlocalmp_pa_t_w4_kernel(tc, F_bytes, F_scale, W1_words, W1_scales, b1
         fsc = const.tile([P, 4], F32)
         nc.sync.dma_start(out=fsc[:], in_=F_scale.rearrange("a c (p t) -> p (a c t)", t=4))
         w1raw = const.tile([P, 2, 2 * C], U8, align_bytes=64)
+        for g in range(2):
+            nc.sync.dma_start(out=w1raw[:, g, :].bitcast(I32), in_=W1_words[g].bitcast(I32))
         w1sraw = const.tile([P, 2, C], U8, align_bytes=64)
         w2s = const.tile([P, C], U8, align_bytes=64)
         nc.vector.memset(w1sraw[:].rearrange("p g n -> p (g n)").bitcast(I32), 0)
@@ -52,8 +54,6 @@ def tile_nonlocalmp_pa_t_w4_kernel(tc, F_bytes, F_scale, W1_words, W1_scales, b1
         w2s_src = W2_scales.rearrange("g (q r) n -> r q (g n)", r=4)
         for r in range(4):
             nc.sync.dma_start(out=w1sraw[r:P:32, :, :].bitcast(I32), in_=w1s_src[r].bitcast(I32))
-        for g in range(2):
-            nc.sync.dma_start(out=w1raw[:, g, :].bitcast(I32), in_=W1_words[g].bitcast(I32))
         b1raw = const.tile([P, 4], BF16)
         nc.sync.dma_start(out=b1raw[:], in_=b1.rearrange("(p t) -> p t", t=4))
         nc.sync.dma_start(out=fbytes[:, 4 * C : 8 * C], in_=f_src[:, 4 * C : 8 * C])
@@ -63,8 +63,6 @@ def tile_nonlocalmp_pa_t_w4_kernel(tc, F_bytes, F_scale, W1_words, W1_scales, b1
             nc.sync.dma_start(out=w2s[r:P:32, :].bitcast(I32), in_=w2s_src[r].bitcast(I32))
         b2raw = const.tile([P, P], BF16)
         nc.sync.dma_start(out=b2raw[0:4, :], in_=b2.rearrange("(c p) -> c p", p=P))
-        fsc_all = const.tile([P, C], F32)
-        nc.sync.dma_start(out=fsc_all[:], in_=F_scale.rearrange("a c k -> (a c k)").partition_broadcast(P))
 
         ident = const.tile([P, P], F32)
         make_identity(nc, ident[:])
@@ -77,14 +75,14 @@ def tile_nonlocalmp_pa_t_w4_kernel(tc, F_bytes, F_scale, W1_words, W1_scales, b1
         w1p = const.tile([P, 2, 4, 2 * P], U8, align_bytes=64)
         w1s = const.tile([P, 2, 4, P], U8, align_bytes=64)
 
-        def permute_w1(engine, g, t0, t1):
-            engine.tensor_copy(
+        def permute_w1(g, t0, t1):
+            nc.vector.tensor_copy(
                 out=w1p[:, g, t0:t1, :].rearrange("p t (m e) -> p t m e", e=2),
                 in_=w1raw[:, g, :].rearrange("p (m t e) -> p t m e", t=4, e=2)[:, t0:t1],
             )
 
-        def permute_w1_scales(g):
-            nc.gpsimd.tensor_copy(out=w1s[:, g, :, :], in_=w1sraw[:, g, :].rearrange("p (m t) -> p t m", t=4))
+        def permute_w1_scales(g, t0, t1):
+            nc.vector.tensor_copy(out=w1s[:, g, t0:t1, :], in_=w1sraw[:, g, :].rearrange("p (m t) -> p t m", t=4)[:, t0:t1])
 
         fwide = const.tile([P, 8, C], BF16, align_bytes=64)
         fg = const.tile([P, NODES, SETS, 4], BF16, align_bytes=64)
@@ -135,8 +133,6 @@ def tile_nonlocalmp_pa_t_w4_kernel(tc, F_bytes, F_scale, W1_words, W1_scales, b1
                 in_=fs[:, j0:j1, :].bitcast(I32).unsqueeze(2).to_broadcast([P, n, 8, SETS // 4]),
             )
 
-        permute_w1_scales(0)
-        permute_w1_scales(1)
         def repeat_f_dma(j0, j1):
             for j in range(j0, j1):
                 nc.sync.dma_start(out=f8q[:, j, :, :], in_=fq[:, j, :].unsqueeze(1).to_broadcast([P, 8, SETS]))
@@ -145,47 +141,39 @@ def tile_nonlocalmp_pa_t_w4_kernel(tc, F_bytes, F_scale, W1_words, W1_scales, b1
                     in_=fs[:, j, :].bitcast(I32).unsqueeze(1).to_broadcast([P, 8, SETS // 4]),
                 )
 
-        fscaled = const.tile([P, 4, C], BF16, align_bytes=64)
-
-        def transpose_scaled_pair(m, tag):
-            for mm in range(2):
-                nc.gpsimd.tensor_tensor(out=fscaled[:, m + mm - 4, :], in0=fwide[:, m + mm, :], in1=fsc_all[:], op=ALU.mult)
-            xt = ps.tile([P, 2, 2, P], F32, name="xt", tag=tag)
-            for mm in range(2):
-                words = fscaled[:, m + mm - 4, :].bitcast(F32)
-                for u in range(2):
-                    nc.tensor.transpose(xt[:, mm, u, :], words[:, u::2], ident[:])
-            return xt
-
-        def words_out(xt, m):
-            for mm in range(2):
-                jj = 2 * (m + mm)
-                nc.scalar.copy(
-                    out=fg[:, jj : jj + 2, :, :].bitcast(F32),
-                    in_=xt[:, mm, :, :].rearrange("p u (b h) -> p h b u", h=2),
-                )
-
         for m in (2, 3):
             nc.vector.tensor_copy(out=fwide[:, m, :], in_=fbytes[:, m * C : (m + 1) * C].bitcast(FP8))
         for m in (0, 1):
             widen(m)
+        for g in range(2):
+            permute_w1(g, 0, 2)
         xt0 = transpose_pair(0, "l0")
         xt1 = transpose_pair(2, "l1")
         scale_out(xt0, 0)
         scale_out(xt1, 2)
+        permute_w1_scales(0, 0, 2)
         quantise_f(0)
-        for g in range(2):
-            permute_w1(nc.vector, g, 0, 2)
+        permute_w1_scales(1, 0, 2)
         repeat_f(0, 1)
-        for g in range(2):
-            permute_w1(nc.vector, g, 2, 4)
         for m in range(4, 8):
             widen(m)
+        xt2 = transpose_pair(4, "l2")
+        xt3 = transpose_pair(6, "l3")
+        for g in range(2):
+            permute_w1(g, 2, 4)
+            permute_w1_scales(g, 2, 4)
         repeat_f(1, 2)
         repeat_f_dma(2, 4)
         repeat_f_dma(4, 8)
+        scale_out(xt2, 4)
+        scale_out(xt3, 6)
+        quantise_f(1)
+        repeat_f_dma(8, 16)
+
         nb2 = const.tile([P, 4], F32)
         b2x20 = const.tile([P, 4], F32)
+        b2x19 = const.tile([P, 4], F32)
+        b2c = const.tile([P, 4], F32)
 
         def setup_b2():
             nc.scalar.copy(out=b2f[0:4, :], in_=b2raw[0:4, :])
@@ -193,6 +181,8 @@ def tile_nonlocalmp_pa_t_w4_kernel(tc, F_bytes, F_scale, W1_words, W1_scales, b1
             nc.tensor.transpose(bt[:], b2f[:], ident[:])
             nc.scalar.activation(out=nb2[:], in_=bt[:, 0:4], func=ACT.Copy, scale=-1.0)
             nc.scalar.activation(out=b2x20[:], in_=bt[:, 0:4], func=ACT.Copy, scale=20.0)
+            nc.scalar.activation(out=b2x19[:], in_=bt[:, 0:4], func=ACT.Copy, scale=19.0)
+            nc.scalar.copy(out=b2c[:], in_=bt[:, 0:4])
 
         v_of, h_of, hq_of, pn_of, acc_of, lin_of = {}, {}, {}, {}, {}, {}
 
@@ -231,32 +221,38 @@ def tile_nonlocalmp_pa_t_w4_kernel(tc, F_bytes, F_scale, W1_words, W1_scales, b1
             if k == 0:
                 return
             if piece == 0:
-                pos = work.tile([P, 4, BLOCK, 4], BF16, name="pos", bufs=2)
-                neg = work.tile([P, 4, BLOCK, 4], BF16, name="neg", bufs=2)
+                pos = work.tile([P, BLOCK, 4, 4], BF16, name="pos", bufs=2)
+                neg = work.tile([P, BLOCK, 4, 4], BF16, name="neg", bufs=2)
                 pn_of[u] = (pos, neg)
             sign, part = divmod(piece, pieces // 2)
             n = k // (pieces // 2)
             lo = part * n
             nc.scalar.activation(
-                out=pn_of[u][sign][:, :, lo : lo + n, :].rearrange("p e c t -> p (c t) e"),
-                in_=v_of[u][:, BLOCK - k + lo : BLOCK - k + lo + n].rearrange("p c t e -> p (c t) e"),
+                out=pn_of[u][sign][:, lo : lo + n].rearrange("p c e t -> p c t e"),
+                in_=v_of[u][:, BLOCK - k + lo : BLOCK - k + lo + n],
                 func=ACT.Relu,
                 scale=(1.0, -SLOPE)[sign],
             )
 
-        def leaky_direct(u, n0, n1):
-            if n0 == 0:
+        def leaky_direct(u, pair):
+            if pair == 0:
                 h = work.tile([P, 4, UNIT // 4, 4], BF16, name="h", align_bytes=64)
                 h_of[u] = h
-            src = v_of[u][:, n0:n1].rearrange("p c t e -> p (c t) e")
-            nc.vector.scalar_tensor_tensor(out=h_of[u][:, :, n0:n1, :].rearrange("p e c t -> p (c t) e"), in0=src, scalar=SLOPE, in1=src, op0=ALU.mult, op1=ALU.max)
+            d = BLOCK - on_scalar(u)
+            es = slice(2 * pair, 2 * pair + 2)
+            src = v_of[u][:, 0:d, :, es].rearrange("p c t e -> p (c t) e")
+            nc.vector.scalar_tensor_tensor(
+                out=h_of[u][:, es, 0:d, :].rearrange("p e c t -> p (c t) e"), in0=src, scalar=SLOPE, in1=src, op0=ALU.mult, op1=ALU.max
+            )
 
         def leaky_join(u):
             k = on_scalar(u)
             if k == 0:
                 return
             pos, neg = pn_of.pop(u)
-            nc.vector.tensor_tensor(out=h_of[u][:, :, BLOCK - k :, :], in0=pos[:, :, 0:k, :], in1=neg[:, :, 0:k, :], op=ALU.subtract)
+            nc.vector.tensor_tensor(
+                out=h_of[u][:, :, BLOCK - k :, :].rearrange("p e c t -> p c e t"), in0=pos[:, 0:k], in1=neg[:, 0:k], op=ALU.subtract
+            )
 
         def quantise_h(u):
             hq = work.tile([P, UNIT], I32, name="hq", align_bytes=64)
@@ -288,14 +284,24 @@ def tile_nonlocalmp_pa_t_w4_kernel(tc, F_bytes, F_scale, W1_words, W1_scales, b1
                 lin_of[g, c] = lin
             second_matmul(u, c, lin_of[g, c], j == 0, j == NODES - 1)
 
+        last_of = {}
+
+        def by_scalar(u, c):
+            return u == UNITS - 1 and c % 2 == 1
+
         def accumulate(u, c, r):
             g, j = divmod(u, NODES)
             if j == 0 and c == 0:
                 acc = const.tile([P, 4, UNIT], F32, name="acc%d" % g)
                 acc_of[g] = acc
             a = acc_of[g][:, c, :]
-            if j == 0:
-                nc.vector.tensor_scalar(out=a, in0=r[:], scalar1=nb2[:, c : c + 1], scalar2=b2x20[:, c : c + 1], op0=ALU.max, op1=ALU.add)
+            if by_scalar(u, c):
+                last = work.tile([P, UNIT], F32, name="last", bufs=2)
+                nc.scalar.activation(out=last[:], in_=r[:], func=ACT.Relu, bias=b2c[:, c : c + 1], scale=1.0)
+                last_of[g, c] = last
+            elif j == 0:
+                start = b2x19 if by_scalar(u + NODES - 1, c) else b2x20
+                nc.vector.tensor_scalar(out=a, in0=r[:], scalar1=nb2[:, c : c + 1], scalar2=start[:, c : c + 1], op0=ALU.max, op1=ALU.add)
             else:
                 nc.vector.scalar_tensor_tensor(out=a, in0=r[:], scalar=nb2[:, c : c + 1], in1=a, op0=ALU.max, op1=ALU.add)
 
@@ -313,7 +319,11 @@ def tile_nonlocalmp_pa_t_w4_kernel(tc, F_bytes, F_scale, W1_words, W1_scales, b1
             for s in range(4):
                 cols = slice(P * s, P * (s + 1))
                 nc.tensor.matmul(tr[:, s, :], lhsT=quarter_of[g, c][:, cols], rhs=ident[:], is_transpose=True, start=True, stop=False)
-                nc.tensor.matmul(tr[:, s, :], lhsT=acc_of[g][:, c, cols], rhs=ident[:], is_transpose=True, start=False, stop=True)
+                if (g, c) in last_of:
+                    nc.tensor.matmul(tr[:, s, :], lhsT=acc_of[g][:, c, cols], rhs=ident[:], is_transpose=True, start=False, stop=False)
+                    nc.tensor.matmul(tr[:, s, :], lhsT=last_of[g, c][:, cols], rhs=ident[:], is_transpose=True, start=False, stop=True)
+                else:
+                    nc.tensor.matmul(tr[:, s, :], lhsT=acc_of[g][:, c, cols], rhs=ident[:], is_transpose=True, start=False, stop=True)
             st = work.tile([P, 4, P], F32, name="st")
             if on_vector:
                 nc.vector.tensor_scalar(out=st[:], in0=tr[:], scalar1=0.8, scalar2=None, op0=ALU.mult)
@@ -327,51 +337,35 @@ def tile_nonlocalmp_pa_t_w4_kernel(tc, F_bytes, F_scale, W1_words, W1_scales, b1
                 z = first_matmul(u, t, "zr"[t % 2])
                 leave_first(u, t, z)
 
-        def halves(u):
-            d = BLOCK - on_scalar(u)
-            return d // 2, d
-
         setup_b2()
         unit_matmuls(0)
-        leaky_direct(0, 0, BLOCK)
+        leaky_direct(0, 0)
+        leaky_direct(0, 1)
         unit_matmuls(1)
-        scalar_part(1, 0, 2)
-        scalar_part(1, 1, 2)
         quantise_h(0)
         unit_matmuls(2)
-        xt2 = transpose_scaled_pair(4, "l2")
-        xt3 = transpose_scaled_pair(6, "l3")
-        leaky_direct(1, 0, halves(1)[1])
-        leaky_join(1)
+        leaky_direct(1, 0)
+        leaky_direct(1, 1)
 
         for u in range(UNITS):
-            if u == 1:
-                quantise_f(1)
-                repeat_f_dma(8, 12)
-                repeat_f_dma(12, 16)
             w = u + AHEAD
             for c in range(4):
                 if w < UNITS:
                     z = first_matmul(w, c)
                 r = message(u, c)
                 linear_sum(u, c)
-                if w - 1 < UNITS:
-                    scalar_part(w - 1, c, 4)
                 if w < UNITS:
                     leave_first(w, c, z)
-                if u == 0 and c == 0:
-                    words_out(xt2, 4)
-                if u == 0 and c == 1:
-                    words_out(xt3, 6)
+                if w - 1 < UNITS:
+                    scalar_part(w - 1, c, 4)
                 accumulate(u, c, r)
                 if c == 1 and u + 1 < UNITS:
                     quantise_h(u + 1)
                 if w - 1 < UNITS:
-                    a, b = halves(w - 1)
                     if c == 0:
-                        leaky_direct(w - 1, 0, a)
+                        leaky_direct(w - 1, 0)
                     if c == 2:
-                        leaky_direct(w - 1, a, b)
+                        leaky_direct(w - 1, 1)
                     if c == 3:
                         leaky_join(w - 1)
                 if u % NODES == NODES - 1:

@@ -22,8 +22,9 @@ UNIT = 512
 GROUPS = 2
 UNITS = GROUPS * NODES
 AHEAD = 3
+JA = 3
 BLOCK = UNIT // 4
-SPLIT = [0, 0, 32] + [58] * 29
+SPLIT = [0, 0, 32] + [64] * 29
 
 
 def on_scalar(u):
@@ -216,20 +217,18 @@ def tile_nonlocalmp_pa_t_w4_kernel(tc, F_bytes, F_scale, W1_words, W1_scales, b1
                 v_of[u] = v
             nc.scalar.activation(out=v_of[u][:, :, t, :], in_=z[:].rearrange("p (e c) -> p c e", e=4), func=ACT.Identity, bias=b1raw[:, t : t + 1], scale=1.0)
 
-        def scalar_part(u, piece, pieces):
+        def scalar_part(u, piece):
             k = on_scalar(u)
             if k == 0:
                 return
             if piece == 0:
-                pos = work.tile([P, BLOCK, 4, 4], BF16, name="pos", bufs=2)
-                neg = work.tile([P, BLOCK, 4, 4], BF16, name="neg", bufs=2)
+                pos = work.tile([P, 2, BLOCK, 2, 4], BF16, name="pos", bufs=2)
+                neg = work.tile([P, 2, BLOCK, 2, 4], BF16, name="neg", bufs=2)
                 pn_of[u] = (pos, neg)
-            sign, part = divmod(piece, pieces // 2)
-            n = k // (pieces // 2)
-            lo = part * n
+            pair, sign = divmod(piece, 2)
             nc.scalar.activation(
-                out=pn_of[u][sign][:, lo : lo + n].rearrange("p c e t -> p c t e"),
-                in_=v_of[u][:, BLOCK - k + lo : BLOCK - k + lo + n],
+                out=pn_of[u][sign][:, pair, 0:k].rearrange("p c e t -> p c t e"),
+                in_=v_of[u][:, BLOCK - k :, :, 2 * pair : 2 * pair + 2],
                 func=ACT.Relu,
                 scale=(1.0, -SLOPE)[sign],
             )
@@ -245,13 +244,16 @@ def tile_nonlocalmp_pa_t_w4_kernel(tc, F_bytes, F_scale, W1_words, W1_scales, b1
                 out=h_of[u][:, es, 0:d, :].rearrange("p e c t -> p (c t) e"), in0=src, scalar=SLOPE, in1=src, op0=ALU.mult, op1=ALU.max
             )
 
-        def leaky_join(u):
+        def leaky_join(u, pair):
             k = on_scalar(u)
             if k == 0:
                 return
-            pos, neg = pn_of.pop(u)
+            pos, neg = pn_of[u]
             nc.vector.tensor_tensor(
-                out=h_of[u][:, :, BLOCK - k :, :].rearrange("p e c t -> p c e t"), in0=pos[:, 0:k], in1=neg[:, 0:k], op=ALU.subtract
+                out=h_of[u][:, 2 * pair : 2 * pair + 2, BLOCK - k :, :].rearrange("p e c t -> p c e t"),
+                in0=pos[:, pair, 0:k],
+                in1=neg[:, pair, 0:k],
+                op=ALU.subtract,
             )
 
         def quantise_h(u):
@@ -357,7 +359,7 @@ def tile_nonlocalmp_pa_t_w4_kernel(tc, F_bytes, F_scale, W1_words, W1_scales, b1
                 if w < UNITS:
                     leave_first(w, c, z)
                 if w - 1 < UNITS:
-                    scalar_part(w - 1, c, 4)
+                    scalar_part(w - 1, c)
                 accumulate(u, c, r)
                 if c == 1 and u + 1 < UNITS:
                     quantise_h(u + 1)
@@ -366,8 +368,10 @@ def tile_nonlocalmp_pa_t_w4_kernel(tc, F_bytes, F_scale, W1_words, W1_scales, b1
                         leaky_direct(w - 1, 0)
                     if c == 2:
                         leaky_direct(w - 1, 1)
+                    if c == JA:
+                        leaky_join(w - 1, 0)
                     if c == 3:
-                        leaky_join(w - 1)
+                        leaky_join(w - 1, 1)
                 if u % NODES == NODES - 1:
                     leave_linear(u // NODES, c)
                 if NODES <= u < NODES + 4 and c == 3:

from contextlib import ExitStack

import concourse.mybir as mybir
from concourse.masks import make_identity

F32 = mybir.dt.float32
BF16 = mybir.dt.bfloat16
I32 = mybir.dt.int32
U8 = mybir.dt.uint8
FP8 = mybir.dt.float8_e4m3fn
FP8X4 = mybir.dt.float8_e4m3fn_x4
FP4X4 = mybir.dt.float4_e2m1fn_x4
ALU = mybir.AluOpType
ACT = mybir.ActivationFunctionType

P = 128
SETS, NODES, C = 64, 16, 512
SLOPE = 0.2
FLOPS = 2 * SETS * NODES * C * 2 * C + 2 * SETS * NODES * NODES * C * C

UNIT = 512
GROUPS = 2
UNITS = GROUPS * NODES
AHEAD = 3
JA = 3
BLOCK = UNIT // 4
SPLIT = [0, 0, 32] + [64] * 29


def on_scalar(u):
    return SPLIT[u]


def tile_nonlocalmp_pa_t_w4_kernel(tc, F_bytes, F_scale, W1_words, W1_scales, b1, W2_words, W2_scales, b2, out):
    nc = tc.nc
    with ExitStack() as ctx:
        ctx.enter_context(tc.manual_schedule())
        const = ctx.enter_context(tc.tile_pool(name="const", bufs=1))
        work = ctx.enter_context(tc.tile_pool(name="work", bufs=3))
        ps = ctx.enter_context(tc.psum_pool(name="ps", bufs=1))

        fbytes = const.tile([P, 8 * C], U8, align_bytes=64)
        f_src = F_bytes.rearrange("b (h m) k -> (b h) (m k)", h=2)
        nc.sync.dma_start(out=fbytes[:, 0 : 4 * C], in_=f_src[:, 0 : 4 * C])
        fsc = const.tile([P, 4], F32)
        nc.sync.dma_start(out=fsc[:], in_=F_scale.rearrange("a c (p t) -> p (a c t)", t=4))
        w1raw = const.tile([P, 2, 2 * C], U8, align_bytes=64)
        for g in range(2):
            nc.sync.dma_start(out=w1raw[:, g, :].bitcast(I32), in_=W1_words[g].bitcast(I32))
        w1sraw = const.tile([P, 2, C], U8, align_bytes=64)
        w2s = const.tile([P, C], U8, align_bytes=64)
        nc.vector.memset(w1sraw[:].rearrange("p g n -> p (g n)").bitcast(I32), 0)
        nc.vector.memset(w2s[:].bitcast(I32), 0)
        w1s_src = W1_scales.rearrange("g (q r) n -> r q g n", r=4)
        w2s_src = W2_scales.rearrange("g (q r) n -> r q (g n)", r=4)
        for r in range(4):
            nc.sync.dma_start(out=w1sraw[r:P:32, :, :].bitcast(I32), in_=w1s_src[r].bitcast(I32))
        b1raw = const.tile([P, 4], BF16)
        nc.sync.dma_start(out=b1raw[:], in_=b1.rearrange("(p t) -> p t", t=4))
        nc.sync.dma_start(out=fbytes[:, 4 * C : 8 * C], in_=f_src[:, 4 * C : 8 * C])
        w2 = const.tile([P, 2 * C], U8, align_bytes=64)
        nc.sync.dma_start(out=w2[:].bitcast(I32), in_=W2_words[0].bitcast(I32))
        for r in range(4):
            nc.sync.dma_start(out=w2s[r:P:32, :].bitcast(I32), in_=w2s_src[r].bitcast(I32))
        b2raw = const.tile([P, P], BF16)
        nc.sync.dma_start(out=b2raw[0:4, :], in_=b2.rearrange("(c p) -> c p", p=P))

        ident = const.tile([P, P], F32)
        make_identity(nc, ident[:])
        warm = const.tile([P, 1], F32)
        nc.vector.memset(warm[:], 0.0)
        nc.scalar.activation(out=warm[:], in_=warm[:], func=ACT.Relu)
        b2f = const.tile([P, P], F32)
        nc.gpsimd.memset(b2f[:], 0.0)

        w1p = const.tile([P, 2, 4, 2 * P], U8, align_bytes=64)
        w1s = const.tile([P, 2, 4, P], U8, align_bytes=64)

        def permute_w1(g, t0, t1):
            nc.vector.tensor_copy(
                out=w1p[:, g, t0:t1, :].rearrange("p t (m e) -> p t m e", e=2),
                in_=w1raw[:, g, :].rearrange("p (m t e) -> p t m e", t=4, e=2)[:, t0:t1],
            )

        def permute_w1_scales(g, t0, t1):
            nc.vector.tensor_copy(out=w1s[:, g, t0:t1, :], in_=w1sraw[:, g, :].rearrange("p (m t) -> p t m", t=4)[:, t0:t1])

        fwide = const.tile([P, 8, C], BF16, align_bytes=64)
        fg = const.tile([P, NODES, SETS, 4], BF16, align_bytes=64)
        fq = const.tile([P, NODES, SETS], I32, align_bytes=64)
        fs = const.tile([P, NODES, SETS], U8, align_bytes=64)
        f8q = const.tile([P, NODES, 8, SETS], I32, align_bytes=64)
        f8s = const.tile([P, NODES, 8, SETS], U8, align_bytes=64)

        def widen(m):
            nc.scalar.copy(out=fwide[:, m, :], in_=fbytes[:, m * C : (m + 1) * C].bitcast(FP8))

        def transpose_pair(m, tag):
            xt = ps.tile([P, 2, 2, P], F32, name="xt", tag=tag)
            for mm in range(2):
                words = fwide[:, m + mm, :].bitcast(F32)
                for u in range(2):
                    nc.tensor.transpose(xt[:, mm, u, :], words[:, u::2], ident[:])
            return xt

        def scale_out(xt, m):
            for mm in range(2):
                src = xt[:, mm, :, :].bitcast(BF16).rearrange("p u (b h e) -> p h b u e", h=2, e=2)
                sc = fsc[:].rearrange("p (o u e) -> p o u e", o=1, u=2).to_broadcast([P, SETS, 2, 2])
                for h in range(2):
                    nc.vector.tensor_tensor(
                        out=fg[:, 2 * (m + mm) + h, :, :].rearrange("p b (u e) -> p b u e", e=2),
                        in0=src[:, h],
                        in1=sc,
                        op=ALU.mult,
                    )

        def quantise_f(g):
            jj = slice(8 * g, 8 * g + 8)
            nc.vector.quantize_mx(
                out=fq[:, jj, :].rearrange("p j b -> p (j b)").bitcast(FP8X4),
                scales=fs[:, jj, :].rearrange("p j b -> p (j b)"),
                in_=fg[:, jj, :, :].rearrange("p j b t -> p (j b t)"),
            )

        def repeat_f(j0, j1):
            n = j1 - j0
            nc.vector.tensor_copy(
                out=f8q[:, j0:j1, :, :],
                in_=fq[:, j0:j1, :].unsqueeze(2).to_broadcast([P, n, 8, SETS]),
            )
            nc.vector.tensor_copy(
                out=f8s[:, j0:j1, :, :].bitcast(I32),
                in_=fs[:, j0:j1, :].bitcast(I32).unsqueeze(2).to_broadcast([P, n, 8, SETS // 4]),
            )

        def repeat_f_dma(j0, j1):
            for j in range(j0, j1):
                nc.sync.dma_start(out=f8q[:, j, :, :], in_=fq[:, j, :].unsqueeze(1).to_broadcast([P, 8, SETS]))
                nc.sync.dma_start(
                    out=f8s[:, j, :, :].bitcast(I32),
                    in_=fs[:, j, :].bitcast(I32).unsqueeze(1).to_broadcast([P, 8, SETS // 4]),
                )

        for m in (2, 3):
            nc.vector.tensor_copy(out=fwide[:, m, :], in_=fbytes[:, m * C : (m + 1) * C].bitcast(FP8))
        for m in (0, 1):
            widen(m)
        for g in range(2):
            permute_w1(g, 0, 2)
        xt0 = transpose_pair(0, "l0")
        xt1 = transpose_pair(2, "l1")
        scale_out(xt0, 0)
        scale_out(xt1, 2)
        permute_w1_scales(0, 0, 2)
        quantise_f(0)
        permute_w1_scales(1, 0, 2)
        repeat_f(0, 1)
        for m in range(4, 8):
            widen(m)
        xt2 = transpose_pair(4, "l2")
        xt3 = transpose_pair(6, "l3")
        for g in range(2):
            permute_w1(g, 2, 4)
            permute_w1_scales(g, 2, 4)
        repeat_f(1, 2)
        repeat_f_dma(2, 4)
        repeat_f_dma(4, 8)
        scale_out(xt2, 4)
        scale_out(xt3, 6)
        quantise_f(1)
        repeat_f_dma(8, 16)

        nb2 = const.tile([P, 4], F32)
        b2x20 = const.tile([P, 4], F32)
        b2x19 = const.tile([P, 4], F32)
        b2c = const.tile([P, 4], F32)

        def setup_b2():
            nc.scalar.copy(out=b2f[0:4, :], in_=b2raw[0:4, :])
            bt = ps.tile([P, P], F32, name="bt", tag="l0")
            nc.tensor.transpose(bt[:], b2f[:], ident[:])
            nc.scalar.activation(out=nb2[:], in_=bt[:, 0:4], func=ACT.Copy, scale=-1.0)
            nc.scalar.activation(out=b2x20[:], in_=bt[:, 0:4], func=ACT.Copy, scale=20.0)
            nc.scalar.activation(out=b2x19[:], in_=bt[:, 0:4], func=ACT.Copy, scale=19.0)
            nc.scalar.copy(out=b2c[:], in_=bt[:, 0:4])

        v_of, h_of, hq_of, pn_of, acc_of, lin_of = {}, {}, {}, {}, {}, {}

        def first_matmul(u, t, tag="z"):
            g, j = divmod(u, NODES)
            z = ps.tile([P, UNIT], F32, name="z", tag=tag, bufs=2)
            jj = slice(8 * g, 8 * g + 8)
            nc.tensor.matmul_mx(
                out=z[:],
                lhsT=w1p[:, 0, t, :].bitcast(FP4X4),
                lhsT_scale=w1s[:, 0, t, :],
                rhs=fq[:, jj, :].rearrange("p j b -> p (j b)").bitcast(FP8X4),
                rhs_scale=fs[:, jj, :].rearrange("p j b -> p (j b)"),
                start=True,
                stop=False,
            )
            nc.tensor.matmul_mx(
                out=z[:],
                lhsT=w1p[:, 1, t, :].bitcast(FP4X4),
                lhsT_scale=w1s[:, 1, t, :],
                rhs=f8q[:, j, :, :].rearrange("p r b -> p (r b)").bitcast(FP8X4),
                rhs_scale=f8s[:, j, :, :].rearrange("p r b -> p (r b)"),
                start=False,
                stop=True,
            )
            return z

        def leave_first(u, t, z):
            if t == 0:
                v = work.tile([P, UNIT // 4, 4, 4], F32, name="v", align_bytes=64)
                v_of[u] = v
            nc.scalar.activation(out=v_of[u][:, :, t, :], in_=z[:].rearrange("p (e c) -> p c e", e=4), func=ACT.Identity, bias=b1raw[:, t : t + 1], scale=1.0)

        def scalar_part(u, piece):
            k = on_scalar(u)
            if k == 0:
                return
            if piece == 0:
                pos = work.tile([P, 2, BLOCK, 2, 4], BF16, name="pos", bufs=2)
                neg = work.tile([P, 2, BLOCK, 2, 4], BF16, name="neg", bufs=2)
                pn_of[u] = (pos, neg)
            pair, sign = divmod(piece, 2)
            nc.scalar.activation(
                out=pn_of[u][sign][:, pair, 0:k].rearrange("p c e t -> p c t e"),
                in_=v_of[u][:, BLOCK - k :, :, 2 * pair : 2 * pair + 2],
                func=ACT.Relu,
                scale=(1.0, -SLOPE)[sign],
            )

        def leaky_direct(u, pair):
            if pair == 0:
                h = work.tile([P, 4, UNIT // 4, 4], BF16, name="h", align_bytes=64)
                h_of[u] = h
            d = BLOCK - on_scalar(u)
            es = slice(2 * pair, 2 * pair + 2)
            src = v_of[u][:, 0:d, :, es].rearrange("p c t e -> p (c t) e")
            nc.vector.scalar_tensor_tensor(
                out=h_of[u][:, es, 0:d, :].rearrange("p e c t -> p (c t) e"), in0=src, scalar=SLOPE, in1=src, op0=ALU.mult, op1=ALU.max
            )

        def leaky_join(u, pair):
            k = on_scalar(u)
            if k == 0:
                return
            pos, neg = pn_of[u]
            nc.vector.tensor_tensor(
                out=h_of[u][:, 2 * pair : 2 * pair + 2, BLOCK - k :, :].rearrange("p e c t -> p c e t"),
                in0=pos[:, pair, 0:k],
                in1=neg[:, pair, 0:k],
                op=ALU.subtract,
            )

        def quantise_h(u):
            hq = work.tile([P, UNIT], I32, name="hq", align_bytes=64)
            hs = work.tile([P, UNIT], U8, name="hs", align_bytes=64)
            hq_of[u] = (hq, hs)
            nc.vector.quantize_mx(out=hq[:].bitcast(FP8X4), scales=hs[:], in_=h_of.pop(u)[:].rearrange("p e c t -> p (e c t)"))

        def second_matmul(u, c, to, start, stop):
            hq, hs = hq_of[u]
            nc.tensor.matmul_mx(
                out=to[:],
                lhsT=w2[:, 2 * P * c : 2 * P * (c + 1)].bitcast(FP4X4),
                lhsT_scale=w2s[:, P * c : P * (c + 1)],
                rhs=hq[:].bitcast(FP8X4),
                rhs_scale=hs[:],
                start=start,
                stop=stop,
            )

        def message(u, c):
            r = ps.tile([P, UNIT], F32, name="r", tag="r", bufs=2)
            second_matmul(u, c, r, True, True)
            return r

        def linear_sum(u, c):
            g, j = divmod(u, NODES)
            if j == 0:
                lin = ps.tile([P, UNIT], F32, name="lin", tag="l%d" % c)
                lin_of[g, c] = lin
            second_matmul(u, c, lin_of[g, c], j == 0, j == NODES - 1)

        last_of = {}

        def by_scalar(u, c):
            return u == UNITS - 1 and c % 2 == 1

        def accumulate(u, c, r):
            g, j = divmod(u, NODES)
            if j == 0 and c == 0:
                acc = const.tile([P, 4, UNIT], F32, name="acc%d" % g)
                acc_of[g] = acc
            a = acc_of[g][:, c, :]
            if by_scalar(u, c):
                last = work.tile([P, UNIT], F32, name="last", bufs=2)
                nc.scalar.activation(out=last[:], in_=r[:], func=ACT.Relu, bias=b2c[:, c : c + 1], scale=1.0)
                last_of[g, c] = last
            elif j == 0:
                start = b2x19 if by_scalar(u + NODES - 1, c) else b2x20
                nc.vector.tensor_scalar(out=a, in0=r[:], scalar1=nb2[:, c : c + 1], scalar2=start[:, c : c + 1], op0=ALU.max, op1=ALU.add)
            else:
                nc.vector.scalar_tensor_tensor(out=a, in0=r[:], scalar=nb2[:, c : c + 1], in1=a, op0=ALU.max, op1=ALU.add)

        quarter_of = {}

        def leave_linear(g, c):
            quarter = work.tile([P, UNIT], F32, name="quarter", bufs=4)
            nc.scalar.activation(out=quarter[:], in_=lin_of[g, c][:], func=ACT.Copy, scale=0.25)
            quarter_of[g, c] = quarter

        out_v = out.rearrange("b (h q s) c -> h q b s c", h=2, q=2)

        def finish(g, c, tag, bufs, on_vector):
            tr = ps.tile([P, 4, P], F32, name="tr", tag=tag, bufs=bufs)
            for s in range(4):
                cols = slice(P * s, P * (s + 1))
                nc.tensor.matmul(tr[:, s, :], lhsT=quarter_of[g, c][:, cols], rhs=ident[:], is_transpose=True, start=True, stop=False)
                if (g, c) in last_of:
                    nc.tensor.matmul(tr[:, s, :], lhsT=acc_of[g][:, c, cols], rhs=ident[:], is_transpose=True, start=False, stop=False)
                    nc.tensor.matmul(tr[:, s, :], lhsT=last_of[g, c][:, cols], rhs=ident[:], is_transpose=True, start=False, stop=True)
                else:
                    nc.tensor.matmul(tr[:, s, :], lhsT=acc_of[g][:, c, cols], rhs=ident[:], is_transpose=True, start=False, stop=True)
            st = work.tile([P, 4, P], F32, name="st")
            if on_vector:
                nc.vector.tensor_scalar(out=st[:], in0=tr[:], scalar1=0.8, scalar2=None, op0=ALU.mult)
            else:
                nc.scalar.activation(out=st[:], in_=tr[:], func=ACT.Copy, scale=0.8)
            for h in range(2):
                nc.sync.dma_start(out=out_v[h, g][:, :, P * c : P * (c + 1)], in_=st[64 * h : 64 * h + 64, :, :])

        def unit_matmuls(u):
            for t in range(4):
                z = first_matmul(u, t, "zr"[t % 2])
                leave_first(u, t, z)

        setup_b2()
        unit_matmuls(0)
        leaky_direct(0, 0)
        leaky_direct(0, 1)
        unit_matmuls(1)
        quantise_h(0)
        unit_matmuls(2)
        leaky_direct(1, 0)
        leaky_direct(1, 1)

        for u in range(UNITS):
            w = u + AHEAD
            for c in range(4):
                if w < UNITS:
                    z = first_matmul(w, c)
                r = message(u, c)
                linear_sum(u, c)
                if w < UNITS:
                    leave_first(w, c, z)
                if w - 1 < UNITS:
                    scalar_part(w - 1, c)
                accumulate(u, c, r)
                if c == 1 and u + 1 < UNITS:
                    quantise_h(u + 1)
                if w - 1 < UNITS:
                    if c == 0:
                        leaky_direct(w - 1, 0)
                    if c == 2:
                        leaky_direct(w - 1, 1)
                    if c == JA:
                        leaky_join(w - 1, 0)
                    if c == 3:
                        leaky_join(w - 1, 1)
                if u % NODES == NODES - 1:
                    leave_linear(u // NODES, c)
                if NODES <= u < NODES + 4 and c == 3:
                    finish(0, u - NODES, "r", 2, False)
        for c in range(4):
            finish(1, c, ("r", "z")[c % 2], 2, c % 2 == 1)
